import numpy as np
import ml_dtypes

BF16 = ml_dtypes.bfloat16


def bf(x):
    return np.asarray(x, np.float32).astype(BF16)


def f32(x):
    return np.asarray(x, np.float32)


def f64(x):
    return np.asarray(x).astype(np.float64)


def striped(idx):
    return np.tile(idx.reshape(-1, 16).T, (8, 1))


C, S, N = 128, 2048, 256
MOM = 0.5


def setup_inputs():
    return {"memory": f32(np.random.standard_normal((C, S))), "v": f32(np.random.standard_normal((C, N))), "offs": striped(np.random.permutation(S)[:N])}


def reference(memory, v, offs):
    idx = offs[:16].T.reshape(-1)
    p = MOM * f64(memory)[:, idx] + (1.0 - MOM) * f64(v)
    return p / np.sqrt(np.sum(p * p, axis=0, keepdims=True))

@@ -1,0 +1,57 @@
+import concourse.mybir as mybir
+
+C, S, N = 128, 2048, 256
+F32, BF16, U16 = mybir.dt.float32, mybir.dt.bfloat16, mybir.dt.uint16
+ADD, MULT = mybir.AluOpType.add, mybir.AluOpType.mult
+ACT = mybir.ActivationFunctionType
+
+FLOPS = 6 * C * N
+
+PIECE = N // 4
+PIECES = N // PIECE
+BURST = 256
+
+
+def tile_contrastmemory_kernel(tc, memory, v, offs, out):
+    nc = tc.nc
+    with (
+        tc.tile_pool(name="held", bufs=1) as held,
+        tc.psum_pool(name="psum", bufs=1) as psum,
+    ):
+        offsets = held.tile([C, N // 16], U16, name="offsets")
+        nc.sync.dma_start(offsets[:], offs)
+        bank = held.tile([C, S], F32, name="bank", align_bytes=BURST)
+        nc.scalar.dma_start(bank[:], memory)
+        fresh = [held.tile([C, N // 2], F32, name=f"fresh_{h}", align_bytes=BURST) for h in range(2)]
+        nc.sync.dma_start(fresh[0][:], v[:, : N // 2])
+        nc.scalar.dma_start(fresh[1][:], v[:, N // 2 :])
+
+        ones = held.tile([C, C], BF16, name="ones")
+        nc.vector.memset(ones[:], 1.0)
+
+        scratch = held.tile([C, 1], F32, name="scratch")
+        nc.vector.memset(scratch[:], 1.0)
+        nc.scalar.activation(scratch[:], scratch[:], ACT.Abs_reciprocal_sqrt)
+
+        blend = held.tile([C, N], F32, name="blend")
+        squares = held.tile([C, N], BF16, name="squares")
+        inverse = held.tile([C, N], F32, name="inverse")
+        unit = held.tile([C, N], F32, name="unit", align_bytes=BURST)
+        length2 = [psum.tile([C, PIECE], F32, name=f"length2_{k}") for k in range(PIECES)]
+        columns = [slice(k * PIECE, (k + 1) * PIECE) for k in range(PIECES)]
+
+        for k in range(PIECES):
+            picked = bank[:].indirect(offsets[:, k * PIECE // 16 : (k + 1) * PIECE // 16])
+            new = fresh[k // 2][:, (k % 2) * PIECE : (k % 2 + 1) * PIECE]
+            nc.vector.tensor_tensor(blend[:, columns[k]], picked, new, ADD)
+        for k in range(PIECES // 2):
+            nc.scalar.activation(squares[:, columns[k]], blend[:, columns[k]], ACT.Square)
+        for k in range(PIECES // 2, PIECES):
+            nc.vector.tensor_tensor(squares[:, columns[k]], blend[:, columns[k]], blend[:, columns[k]], MULT)
+        for k in range(PIECES):
+            nc.tensor.matmul(length2[k][:], ones[:], squares[:, columns[k]], start=True, stop=True)
+        for k in range(PIECES):
+            nc.scalar.activation(inverse[:, columns[k]], length2[k][:], ACT.Abs_reciprocal_sqrt)
+        for k in range(PIECES):
+            nc.vector.tensor_tensor(unit[:, columns[k]], blend[:, columns[k]], inverse[:, columns[k]], MULT)
+            nc.sync.dma_start(out[:, columns[k]], unit[:, columns[k]])

@@ -18,13 +18,13 @@ def tile_contrastmemory_kernel(tc, memory, v, offs, out):
         tc.tile_pool(name="held", bufs=1) as held,
         tc.psum_pool(name="psum", bufs=1) as psum,
     ):
+        bank = held.tile([C, S], F32, name="bank", align_bytes=BURST)
+        nc.sync.dma_start(bank[:], memory)
         offsets = held.tile([C, N // 16], U16, name="offsets")
         nc.sync.dma_start(offsets[:], offs)
-        bank = held.tile([C, S], F32, name="bank", align_bytes=BURST)
-        nc.scalar.dma_start(bank[:], memory)
         fresh = [held.tile([C, N // 2], F32, name=f"fresh_{h}", align_bytes=BURST) for h in range(2)]
         nc.sync.dma_start(fresh[0][:], v[:, : N // 2])
-        nc.scalar.dma_start(fresh[1][:], v[:, N // 2 :])
+        nc.sync.dma_start(fresh[1][:], v[:, N // 2 :])
 
         ones = held.tile([C, C], BF16, name="ones")
         nc.vector.memset(ones[:], 1.0)

@@ -40,18 +40,21 @@ def tile_contrastmemory_kernel(tc, memory, v, offs, out):
         length2 = [psum.tile([C, PIECE], F32, name=f"length2_{k}") for k in range(PIECES)]
         columns = [slice(k * PIECE, (k + 1) * PIECE) for k in range(PIECES)]
 
-        for k in range(PIECES):
-            picked = bank[:].indirect(offsets[:, k * PIECE // 16 : (k + 1) * PIECE // 16])
-            new = fresh[k // 2][:, (k % 2) * PIECE : (k % 2 + 1) * PIECE]
-            nc.vector.tensor_tensor(blend[:, columns[k]], picked, new, ADD)
-        for k in range(PIECES // 2):
-            nc.scalar.activation(squares[:, columns[k]], blend[:, columns[k]], ACT.Square)
-        for k in range(PIECES // 2, PIECES):
-            nc.vector.tensor_tensor(squares[:, columns[k]], blend[:, columns[k]], blend[:, columns[k]], MULT)
+        for start, stop in ((0, 128), (128, 192), (192, 256)):
+            picked = bank[:].indirect(offsets[:, start // 16 : stop // 16])
+            half = start // (N // 2)
+            new = fresh[half][:, start - half * N // 2 : stop - half * N // 2]
+            nc.vector.tensor_tensor(blend[:, start:stop], picked, new, ADD)
+        for start, stop in ((0, 64), (64, 128)):
+            nc.scalar.activation(squares[:, start:stop], blend[:, start:stop], ACT.Square)
+        for start, stop in ((128, 192), (192, 256)):
+            part = blend[:, start:stop]
+            nc.vector.tensor_tensor(squares[:, start:stop], part, part, MULT)
         for k in range(PIECES):
             nc.tensor.matmul(length2[k][:], ones[:], squares[:, columns[k]], start=True, stop=True)
         for k in range(PIECES):
             nc.scalar.activation(inverse[:, columns[k]], length2[k][:], ACT.Abs_reciprocal_sqrt)
         for k in range(PIECES):
             nc.vector.tensor_tensor(unit[:, columns[k]], blend[:, columns[k]], inverse[:, columns[k]], MULT)
-            nc.sync.dma_start(out[:, columns[k]], unit[:, columns[k]])
+        for start, stop in ((0, 128), (128, 256)):
+            nc.sync.dma_start(out[:, start:stop], unit[:, start:stop])

@@ -23,7 +23,7 @@ def tile_contrastmemory_kernel(tc, memory, v, offs, out):
         offsets = held.tile([C, N // 16], U16, name="offsets")
         nc.sync.dma_start(offsets[:], offs)
         fresh = [held.tile([C, N // 2], F32, name=f"fresh_{h}", align_bytes=BURST) for h in range(2)]
-        nc.sync.dma_start(fresh[0][:], v[:, : N // 2])
+        nc.scalar.dma_start(fresh[0][:], v[:, : N // 2])
         nc.sync.dma_start(fresh[1][:], v[:, N // 2 :])
 
         ones = held.tile([C, C], BF16, name="ones")
@@ -56,5 +56,5 @@ def tile_contrastmemory_kernel(tc, memory, v, offs, out):
             nc.scalar.activation(inverse[:, columns[k]], length2[k][:], ACT.Abs_reciprocal_sqrt)
         for k in range(PIECES):
             nc.vector.tensor_tensor(unit[:, columns[k]], blend[:, columns[k]], inverse[:, columns[k]], MULT)
-        for start, stop in ((0, 128), (128, 256)):
+        for start, stop in ((0, 128), (128, 192), (192, 256)):
             nc.sync.dma_start(out[:, start:stop], unit[:, start:stop])

import concourse.mybir as mybir

C, S, N = 128, 2048, 256
F32, BF16, U16 = mybir.dt.float32, mybir.dt.bfloat16, mybir.dt.uint16
ADD, MULT = mybir.AluOpType.add, mybir.AluOpType.mult
ACT = mybir.ActivationFunctionType

FLOPS = 6 * C * N

PIECE = N // 4
PIECES = N // PIECE
BURST = 256


def tile_contrastmemory_kernel(tc, memory, v, offs, out):
    nc = tc.nc
    with (
        tc.tile_pool(name="held", bufs=1) as held,
        tc.psum_pool(name="psum", bufs=1) as psum,
    ):
        bank = held.tile([C, S], F32, name="bank", align_bytes=BURST)
        nc.sync.dma_start(bank[:], memory)
        offsets = held.tile([C, N // 16], U16, name="offsets")
        nc.sync.dma_start(offsets[:], offs)
        fresh = [held.tile([C, N // 2], F32, name=f"fresh_{h}", align_bytes=BURST) for h in range(2)]
        nc.scalar.dma_start(fresh[0][:], v[:, : N // 2])
        nc.sync.dma_start(fresh[1][:], v[:, N // 2 :])

        ones = held.tile([C, C], BF16, name="ones")
        nc.vector.memset(ones[:], 1.0)

        scratch = held.tile([C, 1], F32, name="scratch")
        nc.vector.memset(scratch[:], 1.0)
        nc.scalar.activation(scratch[:], scratch[:], ACT.Abs_reciprocal_sqrt)

        blend = held.tile([C, N], F32, name="blend")
        squares = held.tile([C, N], BF16, name="squares")
        inverse = held.tile([C, N], F32, name="inverse")
        unit = held.tile([C, N], F32, name="unit", align_bytes=BURST)
        length2 = [psum.tile([C, PIECE], F32, name=f"length2_{k}") for k in range(PIECES)]
        columns = [slice(k * PIECE, (k + 1) * PIECE) for k in range(PIECES)]

        for start, stop in ((0, 128), (128, 192), (192, 256)):
            picked = bank[:].indirect(offsets[:, start // 16 : stop // 16])
            half = start // (N // 2)
            new = fresh[half][:, start - half * N // 2 : stop - half * N // 2]
            nc.vector.tensor_tensor(blend[:, start:stop], picked, new, ADD)
        for start, stop in ((0, 64), (64, 128)):
            nc.scalar.activation(squares[:, start:stop], blend[:, start:stop], ACT.Square)
        for start, stop in ((128, 192), (192, 256)):
            part = blend[:, start:stop]
            nc.vector.tensor_tensor(squares[:, start:stop], part, part, MULT)
        for k in range(PIECES):
            nc.tensor.matmul(length2[k][:], ones[:], squares[:, columns[k]], start=True, stop=True)
        for k in range(PIECES):
            nc.scalar.activation(inverse[:, columns[k]], length2[k][:], ACT.Abs_reciprocal_sqrt)
        for k in range(PIECES):
            nc.vector.tensor_tensor(unit[:, columns[k]], blend[:, columns[k]], inverse[:, columns[k]], MULT)
        for start, stop in ((0, 128), (128, 192), (192, 256)):
            nc.sync.dma_start(out[:, start:stop], unit[:, start:stop])
